import numpy as np
import ml_dtypes


def mxq(x, axis, fmt="e4m3"):
    dtype, down = {"e4m3": (ml_dtypes.float8_e4m3fn, 7), "e5m2": (ml_dtypes.float8_e5m2, 14)}[fmt]
    v = np.moveaxis(np.asarray(x, np.float32).astype(ml_dtypes.bfloat16).astype(np.float64), axis, -1)
    blocks = v.reshape(v.shape[:-1] + (-1, 32))
    amax = np.abs(blocks).max(-1, keepdims=True)
    byte = np.maximum(np.where(amax > 0, np.frexp(amax)[1] - 1 + 127, 0) - down, 1)
    scale = np.exp2(byte - 127.0)
    codes = (blocks / scale).astype(np.float32).astype(dtype).astype(np.float64)
    return np.moveaxis((codes * scale).reshape(v.shape), -1, axis)


WIDE = False


def mx_kscale(k):
    if not WIDE:
        return np.ones(k)
    levels = np.array([10, -10, 5, -5, 0])
    if k % 512:
        return np.exp2(np.random.permutation(np.resize(levels, k // 32))).repeat(32)
    a = np.empty((k // 512, 16))
    for p in range(k // 512):
        a[p, :8] = np.random.permutation(np.resize(levels, 8))
        for g in range(8):
            far = levels[np.abs(levels - a[p, g]) >= 10]
            a[p, g + 8] = far[np.random.randint(len(far))]
    return np.exp2(a.ravel()).repeat(32)


BF16 = ml_dtypes.bfloat16


def bf(x):
    return np.asarray(x, np.float32).astype(BF16)


def f64(x):
    return np.asarray(x).astype(np.float64)


E2M1 = np.array([0.0, 0.5, 1.0, 1.5, 2.0, 3.0, 4.0, 6.0, -0.0, -0.5, -1.0, -1.5, -2.0, -3.0, -4.0, -6.0])


def pack_weight(w, fmt):
    k, n = w.shape
    w = f64(bf(w)).reshape(k // 32, 32, n)
    amax = np.abs(w).max(1)
    if fmt == "e4m3":
        byte = np.frexp(amax)[1] - 1 + 127 - 7
    else:
        mant, ex = np.frexp(amax / 6.0)
        byte = np.where(mant > 0.5, ex, ex - 1) + 127
    byte = np.clip(np.where(amax > 0, byte, 1), 1, 254)
    scaled = (w * np.exp2(127.0 - byte)[:, None, :]).reshape(k, n).astype(np.float32)
    by_word = np.ascontiguousarray(scaled.reshape(k // 512, 128, 4, n).transpose(0, 1, 3, 2))
    if fmt == "e4m3":
        words = by_word.astype(ml_dtypes.float8_e4m3fn).view(np.uint8)
    else:
        c = by_word.astype(ml_dtypes.float4_e2m1fn).view(np.uint8) & 0xF
        words = c[..., 0::2] | (c[..., 1::2] << 4)
    return np.ascontiguousarray(words), np.ascontiguousarray(byte.astype(np.uint8).reshape(k // 512, 16, n))


def unpack_weight(words, scales, fmt):
    g, p, n, _ = words.shape
    if fmt == "e4m3":
        vals = np.ascontiguousarray(words).view(ml_dtypes.float8_e4m3fn).astype(np.float64)
    else:
        nib = np.empty((g, p, n, 4), np.uint8)
        nib[..., 0::2] = words & 0xF
        nib[..., 1::2] = words >> 4
        vals = E2M1[nib]
    vals = vals * np.repeat(np.exp2(scales.astype(np.float64) - 127.0), 8, axis=1)[..., None]
    return vals.transpose(0, 1, 3, 2).reshape(g * 512, n)


B, T, C, QLR, H, R, KVL, VD = 4, 1024, 1024, 1536, 4, 128, 512, 128
THETA = 10000.0
EPS = 1e-6
HALF = R // 2


def rms_norm(v, w):
    return v / np.sqrt(np.mean(v * v, axis=-1, keepdims=True) + EPS) * w


def rope_cos_sin():
    inv = 1.0 / THETA ** (np.arange(HALF) / HALF)
    ang = np.arange(T)[:, None] * inv
    return np.cos(ang), np.sin(ang)


def apply_rot(v, cos, sin):
    vr, vi = v[..., 0::2], v[..., 1::2]
    c = cos[None, :, None, :]
    s = sin[None, :, None, :]
    return np.stack([vr * c - vi * s, vr * s + vi * c], axis=-1).reshape(v.shape)


def draw0():
    s, t = mx_kscale(C), mx_kscale(KVL)
    x = bf(np.random.standard_normal((B, T, C)) * s)
    w_kva_words, w_kva_scales = pack_weight((np.random.standard_normal((KVL + R, C)) / np.sqrt(C) / s).T, "e4m3")
    kva_norm_w = bf((1.0 + 0.1 * np.random.standard_normal(KVL)) * t)
    w_kvb_words, w_kvb_scales = pack_weight((np.random.standard_normal((H * (R + VD), KVL)) / np.sqrt(KVL) / t).T, "e4m3")
    return {"x": x,
            "w_kva_words": w_kva_words,
            "w_kva_scales": w_kva_scales,
            "kva_norm_w": kva_norm_w,
            "w_kvb_words": w_kvb_words,
            "w_kvb_scales": w_kvb_scales}


def core(x, w_kva_words, w_kva_scales, kva_norm_w, w_kvb_words, w_kvb_scales):
    kv_a = mxq(f64(x), 2, "e4m3") @ unpack_weight(w_kva_words, w_kva_scales, "e4m3")
    kv_c = rms_norm(kv_a[..., :KVL], f64(kva_norm_w))
    k_rope_raw = kv_a[..., KVL:]
    kv = (mxq(kv_c, 2, "e4m3") @ unpack_weight(w_kvb_words, w_kvb_scales, "e4m3")).reshape(B, T, H, R + VD)
    k_content, v = kv[..., :R], kv[..., R:]
    k_rope = np.broadcast_to(k_rope_raw[:, :, None, :], (B, T, H, R))
    cos, sin = rope_cos_sin()
    k = np.concatenate([k_content, apply_rot(k_rope, cos, sin)], axis=-1)
    return k, v


def e4m3fn_bytes(y):
    return np.clip(np.asarray(y, np.float64), -448.0, 448.0).astype(np.float32).astype(ml_dtypes.float8_e4m3fn).view(np.uint8)


def e4m3fn_values(b):
    return np.asarray(b, np.uint8).view(ml_dtypes.float8_e4m3fn).astype(np.float64)


def setup_inputs():
    d = draw0()
    x0 = np.asarray(d['x']).astype(np.float64)
    s = (np.max(np.abs(x0), axis=(0, 1), keepdims=True) / 448.0).astype(np.float32)
    out = {}
    for k, v in d.items():
        if k == 'x':
            out['x_bytes'] = e4m3fn_bytes(x0 / s.astype(np.float64))
            out['x_scale'] = s
        else:
            out[k] = v
    return out


def reference(x_bytes, x_scale, w_kva_words, w_kva_scales, kva_norm_w, w_kvb_words, w_kvb_scales):
    return core(e4m3fn_values(x_bytes) * x_scale.astype(np.float64), w_kva_words, w_kva_scales, kva_norm_w, w_kvb_words, w_kvb_scales)

@@ -1,0 +1,347 @@
+import math
+from contextlib import ExitStack
+
+import concourse.mybir as mybir
+from concourse.masks import make_identity
+
+F32 = mybir.dt.float32
+BF16 = mybir.dt.bfloat16
+I32 = mybir.dt.int32
+U32 = mybir.dt.uint32
+U8 = mybir.dt.uint8
+FP8 = mybir.dt.float8_e4m3fn
+FP8X4 = mybir.dt.float8_e4m3fn_x4
+ACT = mybir.ActivationFunctionType
+ALU = mybir.AluOpType
+
+B, T, C, H, R, KVL, VD = 4, 1024, 1024, 4, 128, 512, 128
+THETA = 10000.0
+EPS = 1e-6
+HALF = R // 2
+FLOPS = 2 * B * T * (C * (KVL + R) + KVL * H * (R + VD))
+
+P = 128
+PAIRS = 16
+G1 = C // 512
+
+ORDER = (
+    ("castp", 0, 4),
+    ("c", 0, 1),
+    ("qcp", 0, 0),
+    ("tx", 0, 3),
+    ("tx", 1, 3),
+    ("tc", 0, 1),
+    ("m2A", 1, 0),
+    ("evA", 1, 0),
+    ("qxp", 0, 2),
+    ("c", 1, 1),
+    ("mx1", 0, 2),
+    ("m2B", 0, 0),
+    ("xs", 0, 3),
+    ("tc", 1, 1),
+    ("sq", 0, 2),
+    ("m2A", 0, 0),
+    ("evB", 0, 0),
+    ("rs", 0, 2),
+    ("evA", 0, 0),
+    ("mx1", 1, 2),
+    ("m2B", 1, 0),
+    ("xs", 1, 3),
+    ("ccp", 0, 1),
+    ("sq", 1, 2),
+    ("rc", 0, 2),
+    ("rs", 1, 2),
+    ("evB", 1, 0),
+)
+
+
+def tile_multiheadlatentattention_pb_t_w8_kernel(
+    tc, x_bytes, x_scale, w_kva_words, w_kva_scales, kva_norm_w, w_kvb_words, w_kvb_scales, out_0, out_1
+):
+    nc = tc.nc
+    with ExitStack() as ctx:
+        const = ctx.enter_context(tc.tile_pool(name="const", bufs=1))
+        work = ctx.enter_context(tc.tile_pool(name="work", bufs=2))
+        psum = ctx.enter_context(tc.psum_pool(name="psum", bufs=1))
+        ctx.enter_context(tc.manual_schedule())
+
+        xb = []
+        for g in range(8):
+            xbg = const.tile([P, 4096], U8, name=f"xbytes{g}", align_bytes=64)
+            xb.append(xbg)
+        wa = const.tile([P, G1, KVL + R], U32, name="wa", align_bytes=64)
+        wa_s = const.tile([P, KVL + R], U8, name="wa_s", align_bytes=64)
+        wb = const.tile([P, 2, 512], U32, name="wb", align_bytes=64)
+        wb_s = const.tile([P, 2, 512], U8, name="wb_s", align_bytes=64)
+        xsc = const.tile([P, G1, 4], F32, name="xsc", align_bytes=64)
+        gain = const.tile([P, KVL], BF16, name="gain", align_bytes=64)
+        ident = const.tile([P, P], F32, name="ident", align_bytes=64)
+        eps = const.tile([P, 1], F32, name="eps", align_bytes=64)
+        warm = const.tile([P, 1], F32, name="warm", align_bytes=64)
+
+        def x_src(g):
+            b, q = divmod(g, 2)
+            return x_bytes[b].rearrange("(q p i) k -> q p (i k)", q=2, i=4)[q]
+
+        nc.vector.memset(wa_s[:].bitcast(I32), 0)
+        nc.vector.memset(wb_s[:].rearrange("p s n -> p (s n)").bitcast(I32), 0)
+        nc.vector.memset(eps[:], EPS)
+        nc.vector.memset(warm[:], 0.0)
+        nc.scalar.dma_start(out=xsc[:], in_=x_scale.rearrange("a b (g p t) -> p (a b g) t", g=G1, t=4))
+        nc.scalar.dma_start(out=gain[:], in_=kva_norm_w.partition_broadcast(P))
+        nc.sync.dma_start(out=xb[0][:, 0:1024], in_=x_src(0)[:, 0:1024])
+        nc.sync.dma_start(out=xb[0][:, 1024:2048], in_=x_src(0)[:, 1024:2048])
+        for qd in range(4):
+            nc.sync.dma_start(
+                out=wa_s[32 * qd : 32 * qd + 8, :].bitcast(I32),
+                in_=w_kva_scales[:, 4 * qd : 4 * qd + 4, :].bitcast(I32),
+            )
+        for g in range(G1):
+            nc.sync.dma_start(out=wa[:, g, :].bitcast(I32), in_=w_kva_words[g].rearrange("p n t -> p (n t)").bitcast(I32))
+        nc.sync.dma_start(out=xb[0][:, 2048:4096], in_=x_src(0)[:, 2048:4096])
+        for qd in range(4):
+            for s in range(2):
+                nc.sync.dma_start(
+                    out=wb_s[32 * qd : 32 * qd + 4, s, :].bitcast(I32).rearrange("p (h d) -> p h d", h=H),
+                    in_=w_kvb_scales[0][4 * qd : 4 * qd + 4, :].bitcast(I32).rearrange("r (h s d) -> r s h d", h=H, s=2)[:, s],
+                )
+        for s in range(2):
+            nc.sync.dma_start(
+                out=wb[:, s, :].bitcast(I32).rearrange("p (h d) -> p h d", h=H),
+                in_=w_kvb_words[0].rearrange("p n t -> p (n t)").bitcast(I32).rearrange("p (h s d) -> p s h d", h=H, s=2)[:, s],
+            )
+        for g in range(1, 8):
+            nc.sync.dma_start(out=xb[g][:], in_=x_src(g))
+
+        make_identity(nc, ident[:])
+
+        u = const.tile([P, HALF], F32, name="u")
+        tpos = const.tile([P, 8], F32, name="tpos")
+        turns = const.tile([P, 2, 8 * HALF], F32, name="turns")
+        whole = const.tile([P, 2, 8 * HALF], I32, name="whole")
+        trig = const.tile([P, 2, 8 * HALF], F32, name="trig")
+        nc.gpsimd.iota(tpos[:], pattern=[[512, 2], [1, 4]], base=0, channel_multiplier=4, allow_small_or_imprecise_dtypes=True)
+        nc.gpsimd.memset(u[:, 0:1], 1.0)
+        n = 1
+        while n < HALF:
+            nc.gpsimd.tensor_scalar(out=u[:, n : 2 * n], in0=u[:, 0:n], scalar1=THETA ** (-n / HALF), scalar2=0.0, op0=ALU.mult, op1=ALU.add)
+            n *= 2
+        nc.gpsimd.tensor_scalar(out=tpos[:], in0=tpos[:], scalar1=1.0 / (2.0 * math.pi), scalar2=0.0, op0=ALU.mult, op1=ALU.add)
+        nc.gpsimd.tensor_tensor(
+            out=turns[:, 0, :].rearrange("p (c j) -> p c j", j=HALF),
+            in0=tpos[:].unsqueeze(2).to_broadcast([P, 8, HALF]),
+            in1=u[:].unsqueeze(1).to_broadcast([P, 8, HALF]),
+            op=ALU.mult,
+        )
+        nc.gpsimd.tensor_scalar(out=turns[:, 1, :], in0=turns[:, 0, :], scalar1=1.0, scalar2=0.25, op0=ALU.mult, op1=ALU.add)
+        sin, cos = trig[:, 0, :], trig[:, 1, :]
+
+        def tables():
+            nc.vector.tensor_copy(out=whole[:], in_=turns[:])
+            nc.vector.tensor_tensor(out=turns[:], in0=turns[:], in1=whole[:], op=ALU.subtract)
+            nc.scalar.activation(out=trig[:], in_=turns[:], func=ACT.Sin, scale=2.0 * math.pi)
+            nc.scalar.activation(out=warm[:], in_=warm[:], func=ACT.Abs_reciprocal_sqrt, bias=eps[:])
+
+        xf, xt, xin, xq, xqs = {}, {}, {}, {}, {}
+        lt, rt, cb, ssq, rstd, ct, cin, cq, cqs = {}, {}, {}, {}, {}, {}, {}, {}, {}
+        kvp, ks, vs = {}, {}, {}
+
+        def ok(m):
+            return 0 <= m < PAIRS
+
+        def cast(m, a):
+            x_f = work.tile([P, 2048], BF16, name="x_f", bufs=4, align_bytes=64)
+            xf[m] = x_f
+            src = xb[m // 2][:, 2048 * (m % 2) : 2048 * (m % 2) + 2048]
+            if m == 0:
+                nc.scalar.copy(out=x_f[:, 0:1024], in_=src[:, 0:1024].bitcast(FP8))
+                nc.vector.tensor_copy(out=x_f[:, 1024:2048], in_=src[:, 1024:2048].bitcast(FP8))
+            else:
+                nc.scalar.copy(out=x_f[:], in_=src.bitcast(FP8))
+
+        def tx(m, a):
+            words = xf[m][:].bitcast(F32)
+            x_t = psum.tile([P, 2, G1, P], F32, name="x_t", bufs=2)
+            xt[m, a] = x_t
+            for g in range(G1):
+                for e in range(2):
+                    base = 512 * a + 256 * g
+                    nc.tensor.transpose(x_t[:, e, g, :], words[:, base + e : base + 256 : 2], ident[:])
+
+        def xs(m, a):
+            if m not in xin:
+                x_in = work.tile([P, 2, G1, P, 4], BF16, name="x_in", bufs=2, align_bytes=64)
+                xin[m] = x_in
+            nc.vector.tensor_tensor(
+                out=xin[m][:, a].rearrange("p g n (u e) -> p g n u e", u=2),
+                in0=xt[m, a][:].rearrange("p u g n -> p (u g n)").bitcast(BF16).rearrange("p (u g n e) -> p g n u e", u=2, g=G1, e=2),
+                in1=xsc[:].unsqueeze(2).to_broadcast([P, G1, P, 4]).rearrange("p g n (u e) -> p g n u e", u=2),
+                op=ALU.mult,
+            )
+
+        def qx(m, a):
+            x_q = work.tile([P, 4, P], U32, name="x_q", bufs=2, align_bytes=64)
+            x_qs = work.tile([P, 4, P], U8, name="x_qs", bufs=2, align_bytes=64)
+            xq[m], xqs[m] = x_q, x_qs
+            nc.vector.quantize_mx(
+                out=x_q[:].rearrange("p a n -> p (a n)").bitcast(FP8X4),
+                scales=x_qs[:].rearrange("p a n -> p (a n)"),
+                in_=xin[m][:].rearrange("p a g n t -> p (a g n t)"),
+            )
+
+        def mx1(m, a):
+            l_t = psum.tile([P, 512], F32, name="l_t", bufs=2)
+            lt[m, a] = l_t
+            if m not in rt:
+                r_t = psum.tile([P, 2, P], F32, name="r_t", bufs=1)
+                rt[m] = r_t
+            r_out = rt[m][:, a, :]
+            for g in range(G1):
+                for out, lo, hi in ((l_t[:], 0, KVL), (r_out, KVL, KVL + R)):
+                    nc.tensor.matmul_mx(
+                        out=out,
+                        lhsT=xq[m][:, 2 * a + g, :].bitcast(FP8X4),
+                        lhsT_scale=xqs[m][:, 2 * a + g, :],
+                        rhs=wa[:, g, lo:hi].bitcast(FP8X4),
+                        rhs_scale=wa_s[4 * g : P, lo:hi],
+                        start=(g == 0),
+                        stop=(g == G1 - 1),
+                    )
+
+        def sq(m, a):
+            if m not in ssq:
+                s_s = work.tile([P, 2], F32, name="s_s", bufs=3)
+                r_s = work.tile([P, 2], F32, name="r_s", bufs=3)
+                ssq[m], rstd[m] = s_s, r_s
+            junk = work.tile([P, 512], BF16, name="junk", bufs=2)
+            nc.scalar.activation(out=junk[:], in_=lt[m, a][:], func=ACT.Square, accum_out=ssq[m][:, a : a + 1])
+
+        def rs(m, a):
+            nc.scalar.activation(
+                out=rstd[m][:, a : a + 1], in_=ssq[m][:, a : a + 1], func=ACT.Abs_reciprocal_sqrt, scale=1.0 / KVL, bias=eps[:]
+            )
+
+        def scale_c(m, a):
+            if m not in cb:
+                c_b = work.tile([P, 1024], BF16, name="c_b", bufs=3, align_bytes=64)
+                cb[m] = c_b
+            nc.vector.scalar_tensor_tensor(
+                out=cb[m][:, 512 * a : 512 * a + 512], in0=lt[m, a][:], scalar=rstd[m][:, a : a + 1], in1=gain[:], op0=ALU.mult, op1=ALU.mult
+            )
+
+        def tcc(m, a):
+            words = cb[m][:].bitcast(F32)
+            if m not in ct:
+                c_t = psum.tile([P, 4, P], F32, name="c_t", bufs=1)
+                ct[m] = c_t
+            for e in range(2):
+                nc.tensor.transpose(ct[m][:, 2 * a + e, :], words[:, 256 * a + e : 256 * a + 256 : 2], ident[:])
+
+        def copy_c(m, a):
+            c_in = work.tile([P, 1024], BF16, name="c_in", bufs=2, align_bytes=64)
+            nc.vector.tensor_copy(
+                out=c_in[:].bitcast(F32).rearrange("p (a n u) -> p a n u", a=2, u=2),
+                in_=ct[m][:].rearrange("p (a u) n -> p a n u", a=2),
+            )
+            cin[m] = c_in
+
+        def qc(m, a):
+            c_q = work.tile([P, 2, P], U32, name="c_q", bufs=3, align_bytes=64)
+            c_qs = work.tile([P, 2, P], U8, name="c_qs", bufs=3, align_bytes=64)
+            cq[m], cqs[m] = c_q, c_qs
+            nc.vector.quantize_mx(
+                out=c_q[:].rearrange("p a n -> p (a n)").bitcast(FP8X4), scales=c_qs[:].rearrange("p a n -> p (a n)"), in_=cin[m][:]
+            )
+
+        def mx2(m, a, s):
+            kv = psum.tile([P, 512], F32, name="kv", bufs=2)
+            kvp[m, a, s] = kv
+            nc.tensor.matmul_mx(
+                out=kv[:],
+                lhsT=cq[m][:, a, :].bitcast(FP8X4),
+                lhsT_scale=cqs[m][:, a, :],
+                rhs=wb[:, s, :].bitcast(FP8X4),
+                rhs_scale=wb_s[:, s, :],
+                start=True,
+                stop=True,
+            )
+
+        def k_tile(m):
+            if m not in ks:
+                k_s = work.tile([P, 2, H, 2 * P], F32, name="k_s", bufs=4)
+                ks[m] = k_s
+            return ks[m]
+
+        def v_tile(m):
+            if m not in vs:
+                v_s = work.tile([P, 2, 512], F32, name="v_s", bufs=4)
+                vs[m] = v_s
+            return vs[m]
+
+        def evac(m, a, s):
+            if s == 0:
+                nc.scalar.copy(out=k_tile(m)[:, a, :, 0:P], in_=kvp[m, a, 0][:].rearrange("p (h d) -> p h d", h=H))
+            else:
+                nc.scalar.copy(out=v_tile(m)[:, a, :], in_=kvp[m, a, 1][:])
+
+        def store(m):
+            b, q = divmod(m // 2, 2)
+            half = m % 2
+            nc.sync.dma_start(
+                out=out_1[b].rearrange("(q p i) h d -> q p (i h d)", q=2, i=4)[q][:, 1024 * half : 1024 * half + 1024],
+                in_=vs[m][:].rearrange("p a n -> p (a n)"),
+            )
+            nc.sync.dma_start(
+                out=out_0[b].rearrange("(q p i) h d -> q p (i h d)", q=2, i=4)[q][:, 2048 * half : 2048 * half + 2048],
+                in_=ks[m][:].rearrange("p a h d -> p (a h d)"),
+            )
+
+        def rc(m, a):
+            r_f = work.tile([P, 256], F32, name="r_f", bufs=2)
+            nc.scalar.copy(out=r_f[:], in_=rt[m][:].rearrange("p i d -> p (i d)"))
+            rope(m, r_f)
+
+        def rope(m, r_f):
+            c0 = 128 * (m % 4)
+            p_c = work.tile([P, 256], F32, name="p_c", bufs=1)
+            p_s = work.tile([P, 256], F32, name="p_s", bufs=1)
+            r_o = work.tile([P, 2, P], F32, name="r_o", bufs=2)
+            r2 = r_f[:].rearrange("p (j e) -> p j e", e=2)
+            for prod, table in ((p_c, cos), (p_s, sin)):
+                nc.gpsimd.tensor_tensor(
+                    out=prod[:].rearrange("p (j e) -> p j e", e=2),
+                    in0=r2,
+                    in1=table[:, c0 : c0 + 128].unsqueeze(2).to_broadcast([P, 128, 2]),
+                    op=ALU.mult,
+                )
+            ro = r_o[:].rearrange("p i d -> p (i d)")
+            nc.gpsimd.tensor_tensor(out=ro[:, 0::2], in0=p_c[:, 0::2], in1=p_s[:, 1::2], op=ALU.subtract)
+            nc.gpsimd.tensor_tensor(out=ro[:, 1::2], in0=p_c[:, 1::2], in1=p_s[:, 0::2], op=ALU.add)
+            for i in range(2):
+                nc.gpsimd.tensor_scalar(
+                    out=k_tile(m)[:, i, :, P : 2 * P],
+                    in0=r_o[:, i, :].unsqueeze(1).to_broadcast([P, H, P]),
+                    scalar1=1.0,
+                    scalar2=0.0,
+                    op0=ALU.mult,
+                    op1=ALU.add,
+                )
+
+        step = {
+            "castp": cast, "tx": tx, "xs": xs, "qxp": qx, "mx1": mx1, "sq": sq, "rs": rs, "c": scale_c, "tc": tcc, "ccp": copy_c, "qcp": qc, "rc": rc,
+            "m2A": lambda m, a: mx2(m, a, 0), "m2B": lambda m, a: mx2(m, a, 1), "evA": lambda m, a: evac(m, a, 0), "evB": lambda m, a: evac(m, a, 1),
+        }
+        lead = max(lag for _, _, lag in ORDER)
+        evs = {}
+        for it in range(-lead, PAIRS):
+            for name, a, lag in ORDER:
+                m = it + lag
+                if not ok(m):
+                    continue
+                step[name](m, a)
+                if name in ("evA", "evB"):
+                    evs[m] = evs.get(m, 0) + 1
+                    if evs[m] == 4:
+                        store(m)
+                if name == "xs" and m == 0 and a == 1:
+                    tables()

@@ -25,33 +25,34 @@ PAIRS = 16
 G1 = C // 512
 
 ORDER = (
-    ("castp", 0, 4),
-    ("c", 0, 1),
-    ("qcp", 0, 0),
-    ("tx", 0, 3),
-    ("tx", 1, 3),
-    ("tc", 0, 1),
-    ("m2A", 1, 0),
-    ("evA", 1, 0),
-    ("qxp", 0, 2),
-    ("c", 1, 1),
-    ("mx1", 0, 2),
-    ("m2B", 0, 0),
-    ("xs", 0, 3),
-    ("tc", 1, 1),
-    ("sq", 0, 2),
-    ("m2A", 0, 0),
-    ("evB", 0, 0),
-    ("rs", 0, 2),
-    ("evA", 0, 0),
-    ("mx1", 1, 2),
-    ("m2B", 1, 0),
+    ("tx", 0, 4),
     ("xs", 1, 3),
-    ("ccp", 0, 1),
-    ("sq", 1, 2),
-    ("rc", 0, 2),
-    ("rs", 1, 2),
+    ("c", 1, 2),
+    ("tx", 1, 4),
+    ("tc", 1, 2),
+    ("qxp", 0, 3),
+    ("qcp", 0, 1),
+    ("evB", 0, 0),
+    ("m2B", 1, 0),
+    ("mx1", 1, 3),
+    ("cast", 0, 5),
     ("evB", 1, 0),
+    ("sq", 1, 3),
+    ("rc", 0, 2),
+    ("m2A", 0, 1),
+    ("castv", 1, 5),
+    ("c", 0, 2),
+    ("tc", 0, 2),
+    ("evA", 0, 1),
+    ("rs", 1, 3),
+    ("mx1", 0, 3),
+    ("m2A", 1, 1),
+    ("m2B", 0, 1),
+    ("ccp", 0, 2),
+    ("sq", 0, 3),
+    ("evA", 1, 1),
+    ("xs", 0, 4),
+    ("rs", 0, 3),
 )
 
 
@@ -150,22 +151,23 @@ def tile_multiheadlatentattention_pb_t_w8_kernel(
             return 0 <= m < PAIRS
 
         def cast(m, a):
-            x_f = work.tile([P, 2048], BF16, name="x_f", bufs=4, align_bytes=64)
-            xf[m] = x_f
-            src = xb[m // 2][:, 2048 * (m % 2) : 2048 * (m % 2) + 2048]
-            if m == 0:
-                nc.scalar.copy(out=x_f[:, 0:1024], in_=src[:, 0:1024].bitcast(FP8))
-                nc.vector.tensor_copy(out=x_f[:, 1024:2048], in_=src[:, 1024:2048].bitcast(FP8))
+            if m not in xf:
+                x_f = work.tile([P, 2, C], BF16, name="x_f", bufs=4, align_bytes=64)
+                xf[m] = x_f
+            first = 2048 * (m % 2) + 1024 * a
+            src = xb[m // 2][:, first : first + C].bitcast(FP8)
+            if a == 0:
+                nc.scalar.copy(out=xf[m][:, a, :], in_=src)
             else:
-                nc.scalar.copy(out=x_f[:], in_=src.bitcast(FP8))
+                nc.vector.tensor_copy(out=xf[m][:, a, :], in_=src)
 
         def tx(m, a):
-            words = xf[m][:].bitcast(F32)
+            words = xf[m][:, a, :].bitcast(F32)
             x_t = psum.tile([P, 2, G1, P], F32, name="x_t", bufs=2)
             xt[m, a] = x_t
             for g in range(G1):
                 for e in range(2):
-                    base = 512 * a + 256 * g
+                    base = 256 * g
                     nc.tensor.transpose(x_t[:, e, g, :], words[:, base + e : base + 256 : 2], ident[:])
 
         def xs(m, a):
@@ -239,7 +241,7 @@ def tile_multiheadlatentattention_pb_t_w8_kernel(
 
         def copy_c(m, a):
             c_in = work.tile([P, 1024], BF16, name="c_in", bufs=2, align_bytes=64)
-            nc.vector.tensor_copy(
+            nc.scalar.copy(
                 out=c_in[:].bitcast(F32).rearrange("p (a n u) -> p a n u", a=2, u=2),
                 in_=ct[m][:].rearrange("p (a u) n -> p a n u", a=2),
             )
@@ -298,7 +300,7 @@ def tile_multiheadlatentattention_pb_t_w8_kernel(
 
         def rc(m, a):
             r_f = work.tile([P, 256], F32, name="r_f", bufs=2)
-            nc.scalar.copy(out=r_f[:], in_=rt[m][:].rearrange("p i d -> p (i d)"))
+            nc.vector.tensor_copy(out=r_f[:], in_=rt[m][:].rearrange("p i d -> p (i d)"))
             rope(m, r_f)
 
         def rope(m, r_f):
@@ -328,7 +330,7 @@ def tile_multiheadlatentattention_pb_t_w8_kernel(
                 )
 
         step = {
-            "castp": cast, "tx": tx, "xs": xs, "qxp": qx, "mx1": mx1, "sq": sq, "rs": rs, "c": scale_c, "tc": tcc, "ccp": copy_c, "qcp": qc, "rc": rc,
+            "cast": cast, "castv": cast, "tx": tx, "xs": xs, "qxp": qx, "mx1": mx1, "sq": sq, "rs": rs, "c": scale_c, "tc": tcc, "ccp": copy_c, "qcp": qc, "rc": rc,
             "m2A": lambda m, a: mx2(m, a, 0), "m2B": lambda m, a: mx2(m, a, 1), "evA": lambda m, a: evac(m, a, 0), "evB": lambda m, a: evac(m, a, 1),
         }
         lead = max(lag for _, _, lag in ORDER)

@@ -25,34 +25,34 @@ PAIRS = 16
 G1 = C // 512
 
 ORDER = (
-    ("tx", 0, 4),
-    ("xs", 1, 3),
-    ("c", 1, 2),
-    ("tx", 1, 4),
-    ("tc", 1, 2),
-    ("qxp", 0, 3),
-    ("qcp", 0, 1),
-    ("evB", 0, 0),
-    ("m2B", 1, 0),
     ("mx1", 1, 3),
-    ("cast", 0, 5),
-    ("evB", 1, 0),
+    ("castp", 0, 6),
     ("sq", 1, 3),
-    ("rc", 0, 2),
     ("m2A", 0, 1),
-    ("castv", 1, 5),
-    ("c", 0, 2),
-    ("tc", 0, 2),
     ("evA", 0, 1),
     ("rs", 1, 3),
-    ("mx1", 0, 3),
-    ("m2A", 1, 1),
     ("m2B", 0, 1),
+    ("c", 1, 3),
+    ("tc", 0, 2),
+    ("evB", 0, 1),
+    ("mx1", 0, 3),
+    ("qxp", 0, 4),
+    ("rm", 0, 3),
+    ("m2A", 1, 1),
     ("ccp", 0, 2),
+    ("tx", 0, 5),
+    ("qcp", 0, 2),
     ("sq", 0, 3),
     ("evA", 1, 1),
-    ("xs", 0, 4),
+    ("ra", 0, 2),
+    ("m2B", 1, 1),
     ("rs", 0, 3),
+    ("tx", 1, 5),
+    ("c", 0, 3),
+    ("xs", 0, 5),
+    ("xs", 1, 5),
+    ("evB", 1, 1),
+    ("tc", 1, 3),
 )
 
 
@@ -120,7 +120,7 @@ def tile_multiheadlatentattention_pb_t_w8_kernel(
         tpos = const.tile([P, 8], F32, name="tpos")
         turns = const.tile([P, 2, 8 * HALF], F32, name="turns")
         whole = const.tile([P, 2, 8 * HALF], I32, name="whole")
-        trig = const.tile([P, 2, 8 * HALF], F32, name="trig")
+        trig = const.tile([P, 4, 2, 256], F32, name="trig")
         nc.gpsimd.iota(tpos[:], pattern=[[512, 2], [1, 4]], base=0, channel_multiplier=4, allow_small_or_imprecise_dtypes=True)
         nc.gpsimd.memset(u[:, 0:1], 1.0)
         n = 1
@@ -135,44 +135,54 @@ def tile_multiheadlatentattention_pb_t_w8_kernel(
             op=ALU.mult,
         )
         nc.gpsimd.tensor_scalar(out=turns[:, 1, :], in0=turns[:, 0, :], scalar1=1.0, scalar2=0.25, op0=ALU.mult, op1=ALU.add)
-        sin, cos = trig[:, 0, :], trig[:, 1, :]
 
         def tables():
             nc.vector.tensor_copy(out=whole[:], in_=turns[:])
             nc.vector.tensor_tensor(out=turns[:], in0=turns[:], in1=whole[:], op=ALU.subtract)
-            nc.scalar.activation(out=trig[:], in_=turns[:], func=ACT.Sin, scale=2.0 * math.pi)
+            nc.scalar.activation(
+                out=trig[:, :, 0, :].rearrange("p s (j e) -> p s j e", e=2),
+                in_=turns[:, 1, :].rearrange("p (s j) -> p s j", s=4).unsqueeze(3).to_broadcast([P, 4, 128, 2]),
+                func=ACT.Sin,
+                scale=2.0 * math.pi,
+            )
+            for e, sign in ((0, 1.0), (1, -1.0)):
+                nc.scalar.activation(
+                    out=trig[:, :, 1, e::2],
+                    in_=turns[:, 0, :].rearrange("p (s j) -> p s j", s=4),
+                    func=ACT.Sin,
+                    scale=sign * 2.0 * math.pi,
+                )
             nc.scalar.activation(out=warm[:], in_=warm[:], func=ACT.Abs_reciprocal_sqrt, bias=eps[:])
 
         xf, xt, xin, xq, xqs = {}, {}, {}, {}, {}
         lt, rt, cb, ssq, rstd, ct, cin, cq, cqs = {}, {}, {}, {}, {}, {}, {}, {}, {}
-        kvp, ks, vs = {}, {}, {}
+        kvp, rp, ks, vs = {}, {}, {}, {}
 
         def ok(m):
             return 0 <= m < PAIRS
 
         def cast(m, a):
-            if m not in xf:
-                x_f = work.tile([P, 2, C], BF16, name="x_f", bufs=4, align_bytes=64)
-                xf[m] = x_f
-            first = 2048 * (m % 2) + 1024 * a
-            src = xb[m // 2][:, first : first + C].bitcast(FP8)
-            if a == 0:
-                nc.scalar.copy(out=xf[m][:, a, :], in_=src)
+            x_f = work.tile([P, 2048], BF16, name="x_f", bufs=4, align_bytes=64)
+            xf[m] = x_f
+            src = xb[m // 2][:, 2048 * (m % 2) : 2048 * (m % 2) + 2048]
+            if m == 0:
+                nc.scalar.copy(out=x_f[:, 0:1024], in_=src[:, 0:1024].bitcast(FP8))
+                nc.vector.tensor_copy(out=x_f[:, 1024:2048], in_=src[:, 1024:2048].bitcast(FP8))
             else:
-                nc.vector.tensor_copy(out=xf[m][:, a, :], in_=src)
+                nc.scalar.copy(out=x_f[:], in_=src.bitcast(FP8))
 
         def tx(m, a):
-            words = xf[m][:, a, :].bitcast(F32)
+            words = xf[m][:].bitcast(F32)
             x_t = psum.tile([P, 2, G1, P], F32, name="x_t", bufs=2)
             xt[m, a] = x_t
             for g in range(G1):
                 for e in range(2):
-                    base = 256 * g
+                    base = 512 * a + 256 * g
                     nc.tensor.transpose(x_t[:, e, g, :], words[:, base + e : base + 256 : 2], ident[:])
 
         def xs(m, a):
             if m not in xin:
-                x_in = work.tile([P, 2, G1, P, 4], BF16, name="x_in", bufs=2, align_bytes=64)
+                x_in = work.tile([P, 2, G1, P, 4], BF16, name="x_in", bufs=3, align_bytes=64)
                 xin[m] = x_in
             nc.vector.tensor_tensor(
                 out=xin[m][:, a].rearrange("p g n (u e) -> p g n u e", u=2),
@@ -182,8 +192,8 @@ def tile_multiheadlatentattention_pb_t_w8_kernel(
             )
 
         def qx(m, a):
-            x_q = work.tile([P, 4, P], U32, name="x_q", bufs=2, align_bytes=64)
-            x_qs = work.tile([P, 4, P], U8, name="x_qs", bufs=2, align_bytes=64)
+            x_q = work.tile([P, 4, P], U32, name="x_q", bufs=3, align_bytes=64)
+            x_qs = work.tile([P, 4, P], U8, name="x_qs", bufs=3, align_bytes=64)
             xq[m], xqs[m] = x_q, x_qs
             nc.vector.quantize_mx(
                 out=x_q[:].rearrange("p a n -> p (a n)").bitcast(FP8X4),
@@ -240,7 +250,7 @@ def tile_multiheadlatentattention_pb_t_w8_kernel(
                 nc.tensor.transpose(ct[m][:, 2 * a + e, :], words[:, 256 * a + e : 256 * a + 256 : 2], ident[:])
 
         def copy_c(m, a):
-            c_in = work.tile([P, 1024], BF16, name="c_in", bufs=2, align_bytes=64)
+            c_in = work.tile([P, 1024], BF16, name="c_in", bufs=3, align_bytes=64)
             nc.scalar.copy(
                 out=c_in[:].bitcast(F32).rearrange("p (a n u) -> p a n u", a=2, u=2),
                 in_=ct[m][:].rearrange("p (a u) n -> p a n u", a=2),
@@ -298,27 +308,24 @@ def tile_multiheadlatentattention_pb_t_w8_kernel(
                 in_=ks[m][:].rearrange("p a h d -> p (a h d)"),
             )
 
-        def rc(m, a):
-            r_f = work.tile([P, 256], F32, name="r_f", bufs=2)
-            nc.vector.tensor_copy(out=r_f[:], in_=rt[m][:].rearrange("p i d -> p (i d)"))
-            rope(m, r_f)
+        def rm(m, a):
+            prod = work.tile([P, 2, 256], F32, name="prod", bufs=3)
+            rp[m] = prod
+            nc.vector.tensor_tensor(
+                out=prod[:],
+                in0=rt[m][:].rearrange("p i d -> p (i d)").unsqueeze(1).to_broadcast([P, 2, 256]),
+                in1=trig[:, m % 4],
+                op=ALU.mult,
+            )
 
-        def rope(m, r_f):
-            c0 = 128 * (m % 4)
-            p_c = work.tile([P, 256], F32, name="p_c", bufs=1)
-            p_s = work.tile([P, 256], F32, name="p_s", bufs=1)
-            r_o = work.tile([P, 2, P], F32, name="r_o", bufs=2)
-            r2 = r_f[:].rearrange("p (j e) -> p j e", e=2)
-            for prod, table in ((p_c, cos), (p_s, sin)):
-                nc.gpsimd.tensor_tensor(
-                    out=prod[:].rearrange("p (j e) -> p j e", e=2),
-                    in0=r2,
-                    in1=table[:, c0 : c0 + 128].unsqueeze(2).to_broadcast([P, 128, 2]),
-                    op=ALU.mult,
-                )
-            ro = r_o[:].rearrange("p i d -> p (i d)")
-            nc.gpsimd.tensor_tensor(out=ro[:, 0::2], in0=p_c[:, 0::2], in1=p_s[:, 1::2], op=ALU.subtract)
-            nc.gpsimd.tensor_tensor(out=ro[:, 1::2], in0=p_c[:, 1::2], in1=p_s[:, 0::2], op=ALU.add)
+        def ra(m, a):
+            r_o = work.tile([P, 2, P], F32, name="r_o", bufs=3)
+            nc.vector.tensor_tensor(
+                out=r_o[:].rearrange("p i (j e) -> p (i j) e", e=2),
+                in0=rp[m][:, 0, :].rearrange("p (j e) -> p j e", e=2),
+                in1=rp[m][:, 1, :].rearrange("p (j e) -> p j e", e=2)[:, :, ::-1],
+                op=ALU.add,
+            )
             for i in range(2):
                 nc.gpsimd.tensor_scalar(
                     out=k_tile(m)[:, i, :, P : 2 * P],
@@ -330,7 +337,7 @@ def tile_multiheadlatentattention_pb_t_w8_kernel(
                 )
 
         step = {
-            "cast": cast, "castv": cast, "tx": tx, "xs": xs, "qxp": qx, "mx1": mx1, "sq": sq, "rs": rs, "c": scale_c, "tc": tcc, "ccp": copy_c, "qcp": qc, "rc": rc,
+            "castp": cast, "tx": tx, "xs": xs, "qxp": qx, "mx1": mx1, "sq": sq, "rs": rs, "c": scale_c, "tc": tcc, "ccp": copy_c, "qcp": qc, "rm": rm, "ra": ra,
             "m2A": lambda m, a: mx2(m, a, 0), "m2B": lambda m, a: mx2(m, a, 1), "evA": lambda m, a: evac(m, a, 0), "evB": lambda m, a: evac(m, a, 1),
         }
         lead = max(lag for _, _, lag in ORDER)

@@ -25,34 +25,34 @@ PAIRS = 16
 G1 = C // 512
 
 ORDER = (
-    ("mx1", 1, 3),
-    ("castp", 0, 6),
-    ("sq", 1, 3),
-    ("m2A", 0, 1),
-    ("evA", 0, 1),
-    ("rs", 1, 3),
-    ("m2B", 0, 1),
-    ("c", 1, 3),
-    ("tc", 0, 2),
-    ("evB", 0, 1),
-    ("mx1", 0, 3),
+    ("ra", 0, 1),
+    ("tc", 1, 2),
     ("qxp", 0, 4),
-    ("rm", 0, 3),
-    ("m2A", 1, 1),
-    ("ccp", 0, 2),
-    ("tx", 0, 5),
-    ("qcp", 0, 2),
-    ("sq", 0, 3),
-    ("evA", 1, 1),
-    ("ra", 0, 2),
-    ("m2B", 1, 1),
-    ("rs", 0, 3),
-    ("tx", 1, 5),
-    ("c", 0, 3),
-    ("xs", 0, 5),
-    ("xs", 1, 5),
     ("evB", 1, 1),
-    ("tc", 1, 3),
+    ("rsp", 0, 3),
+    ("m2A", 1, 1),
+    ("evA", 0, 1),
+    ("xw", 0, 5),
+    ("rm", 0, 3),
+    ("m2B", 0, 1),
+    ("ccp", 0, 2),
+    ("c", 0, 3),
+    ("c", 1, 3),
+    ("xs", 0, 6),
+    ("tx", 1, 5),
+    ("evA", 1, 1),
+    ("evB", 0, 1),
+    ("mx1", 0, 4),
+    ("mx1", 1, 4),
+    ("xw", 1, 5),
+    ("sq", 0, 4),
+    ("tc", 0, 3),
+    ("qcp", 0, 2),
+    ("m2B", 1, 2),
+    ("m2A", 0, 2),
+    ("sq", 1, 4),
+    ("xs", 1, 6),
+    ("tx", 0, 6),
 )
 
 
@@ -72,9 +72,12 @@ def tile_multiheadlatentattention_pb_t_w8_kernel(
             xb.append(xbg)
         wa = const.tile([P, G1, KVL + R], U32, name="wa", align_bytes=64)
         wa_s = const.tile([P, KVL + R], U8, name="wa_s", align_bytes=64)
+        wr = const.tile([P, G1, 2, HALF], U32, name="wr", align_bytes=64)
+        wr_s = const.tile([P, 2, HALF], U8, name="wr_s", align_bytes=64)
         wb = const.tile([P, 2, 512], U32, name="wb", align_bytes=64)
         wb_s = const.tile([P, 2, 512], U8, name="wb_s", align_bytes=64)
-        xsc = const.tile([P, G1, 4], F32, name="xsc", align_bytes=64)
+        xsc = const.tile([P, C], F32, name="xsc", align_bytes=64)
+        xsk = const.tile([P, G1, 4], F32, name="xsk", align_bytes=64)
         gain = const.tile([P, KVL], BF16, name="gain", align_bytes=64)
         ident = const.tile([P, P], F32, name="ident", align_bytes=64)
         eps = const.tile([P, 1], F32, name="eps", align_bytes=64)
@@ -84,12 +87,11 @@ def tile_multiheadlatentattention_pb_t_w8_kernel(
             b, q = divmod(g, 2)
             return x_bytes[b].rearrange("(q p i) k -> q p (i k)", q=2, i=4)[q]
 
-        nc.vector.memset(wa_s[:].bitcast(I32), 0)
-        nc.vector.memset(wb_s[:].rearrange("p s n -> p (s n)").bitcast(I32), 0)
+        nc.gpsimd.memset(wa_s[:].bitcast(I32), 0)
+        nc.gpsimd.memset(wb_s[:].rearrange("p s n -> p (s n)").bitcast(I32), 0)
         nc.vector.memset(eps[:], EPS)
         nc.vector.memset(warm[:], 0.0)
-        nc.scalar.dma_start(out=xsc[:], in_=x_scale.rearrange("a b (g p t) -> p (a b g) t", g=G1, t=4))
-        nc.scalar.dma_start(out=gain[:], in_=kva_norm_w.partition_broadcast(P))
+        nc.scalar.dma_start(out=xsk[:], in_=x_scale.rearrange("a b (g p t) -> p (a b g) t", g=G1, t=4))
         nc.sync.dma_start(out=xb[0][:, 0:1024], in_=x_src(0)[:, 0:1024])
         nc.sync.dma_start(out=xb[0][:, 1024:2048], in_=x_src(0)[:, 1024:2048])
         for qd in range(4):
@@ -100,6 +102,9 @@ def tile_multiheadlatentattention_pb_t_w8_kernel(
         for g in range(G1):
             nc.sync.dma_start(out=wa[:, g, :].bitcast(I32), in_=w_kva_words[g].rearrange("p n t -> p (n t)").bitcast(I32))
         nc.sync.dma_start(out=xb[0][:, 2048:4096], in_=x_src(0)[:, 2048:4096])
+        nc.sync.dma_start(out=xb[1][:], in_=x_src(1))
+        nc.sync.dma_start(out=xsc[:], in_=x_scale.rearrange("a b k -> (a b k)").partition_broadcast(P))
+        nc.sync.dma_start(out=gain[:], in_=kva_norm_w.partition_broadcast(P))
         for qd in range(4):
             for s in range(2):
                 nc.sync.dma_start(
@@ -111,48 +116,49 @@ def tile_multiheadlatentattention_pb_t_w8_kernel(
                 out=wb[:, s, :].bitcast(I32).rearrange("p (h d) -> p h d", h=H),
                 in_=w_kvb_words[0].rearrange("p n t -> p (n t)").bitcast(I32).rearrange("p (h s d) -> p s h d", h=H, s=2)[:, s],
             )
-        for g in range(1, 8):
+        for g in range(2, 8):
             nc.sync.dma_start(out=xb[g][:], in_=x_src(g))
-
-        make_identity(nc, ident[:])
 
         u = const.tile([P, HALF], F32, name="u")
         tpos = const.tile([P, 8], F32, name="tpos")
-        turns = const.tile([P, 2, 8 * HALF], F32, name="turns")
-        whole = const.tile([P, 2, 8 * HALF], I32, name="whole")
-        trig = const.tile([P, 4, 2, 256], F32, name="trig")
+        turns = const.tile([P, 8, HALF], F32, name="turns")
+        whole = const.tile([P, 8, HALF], I32, name="whole")
+        half = const.tile([P, 8, HALF], F32, name="half")
+        half2 = const.tile([P, 8, HALF], F32, name="half2")
+        trig = const.tile([P, 4, 2, 2, 2, HALF], F32, name="trig")
         nc.gpsimd.iota(tpos[:], pattern=[[512, 2], [1, 4]], base=0, channel_multiplier=4, allow_small_or_imprecise_dtypes=True)
-        nc.gpsimd.memset(u[:, 0:1], 1.0)
+        nc.gpsimd.tensor_scalar(out=tpos[:], in0=tpos[:], scalar1=1.0 / (2.0 * math.pi), scalar2=0.0, op0=ALU.mult, op1=ALU.add)
+        make_identity(nc, ident[:])
+        nc.vector.memset(u[:, 0:1], 1.0)
         n = 1
         while n < HALF:
-            nc.gpsimd.tensor_scalar(out=u[:, n : 2 * n], in0=u[:, 0:n], scalar1=THETA ** (-n / HALF), scalar2=0.0, op0=ALU.mult, op1=ALU.add)
+            nc.vector.tensor_scalar(out=u[:, n : 2 * n], in0=u[:, 0:n], scalar1=THETA ** (-n / HALF), scalar2=None, op0=ALU.mult)
             n *= 2
-        nc.gpsimd.tensor_scalar(out=tpos[:], in0=tpos[:], scalar1=1.0 / (2.0 * math.pi), scalar2=0.0, op0=ALU.mult, op1=ALU.add)
-        nc.gpsimd.tensor_tensor(
-            out=turns[:, 0, :].rearrange("p (c j) -> p c j", j=HALF),
-            in0=tpos[:].unsqueeze(2).to_broadcast([P, 8, HALF]),
-            in1=u[:].unsqueeze(1).to_broadcast([P, 8, HALF]),
-            op=ALU.mult,
+        nc.vector.tensor_tensor(
+            out=turns[:], in0=tpos[:].unsqueeze(2).to_broadcast([P, 8, HALF]), in1=u[:].unsqueeze(1).to_broadcast([P, 8, HALF]), op=ALU.mult
         )
-        nc.gpsimd.tensor_scalar(out=turns[:, 1, :], in0=turns[:, 0, :], scalar1=1.0, scalar2=0.25, op0=ALU.mult, op1=ALU.add)
+        nc.vector.tensor_copy(out=whole[:], in_=turns[:])
+        nc.vector.tensor_tensor(out=turns[:], in0=turns[:], in1=whole[:], op=ALU.subtract)
+        nc.scalar.activation(out=warm[:], in_=warm[:], func=ACT.Sin)
 
-        def tables():
-            nc.vector.tensor_copy(out=whole[:], in_=turns[:])
-            nc.vector.tensor_tensor(out=turns[:], in0=turns[:], in1=whole[:], op=ALU.subtract)
-            nc.scalar.activation(
-                out=trig[:, :, 0, :].rearrange("p s (j e) -> p s j e", e=2),
-                in_=turns[:, 1, :].rearrange("p (s j) -> p s j", s=4).unsqueeze(3).to_broadcast([P, 4, 128, 2]),
-                func=ACT.Sin,
-                scale=2.0 * math.pi,
-            )
+        def trig_tables():
+            by_pair = turns[:].rearrange("p (s i) j -> p s i j", i=2)
             for e, sign in ((0, 1.0), (1, -1.0)):
-                nc.scalar.activation(
-                    out=trig[:, :, 1, e::2],
-                    in_=turns[:, 0, :].rearrange("p (s j) -> p s j", s=4),
-                    func=ACT.Sin,
-                    scale=sign * 2.0 * math.pi,
-                )
+                nc.scalar.activation(out=trig[:, :, 1, :, e, :], in_=by_pair, func=ACT.Sin, scale=sign * 2.0 * math.pi)
+            nc.scalar.activation(out=half[:], in_=turns[:], func=ACT.Sin, scale=math.pi)
+            nc.scalar.activation(out=half2[:], in_=half[:], func=ACT.Square)
+            nc.scalar.activation(
+                out=trig[:, :, 0],
+                in_=half2[:].rearrange("p (s i) j -> p s i j", i=2).unsqueeze(3).to_broadcast([P, 4, 2, 2, HALF]),
+                func=ACT.Copy,
+                scale=-2.0,
+                bias=1.0,
+            )
             nc.scalar.activation(out=warm[:], in_=warm[:], func=ACT.Abs_reciprocal_sqrt, bias=eps[:])
+
+        def planar_rope_weights():
+            nc.vector.tensor_copy(out=wr[:].bitcast(I32), in_=wa[:].bitcast(I32)[:, :, KVL:].rearrange("p g (j e) -> p g e j", e=2))
+            nc.vector.tensor_copy(out=wr_s[:], in_=wa_s[:, KVL:].rearrange("p (j e) -> p e j", e=2))
 
         xf, xt, xin, xq, xqs = {}, {}, {}, {}, {}
         lt, rt, cb, ssq, rstd, ct, cin, cq, cqs = {}, {}, {}, {}, {}, {}, {}, {}, {}
@@ -161,34 +167,39 @@ def tile_multiheadlatentattention_pb_t_w8_kernel(
         def ok(m):
             return 0 <= m < PAIRS
 
-        def cast(m, a):
-            x_f = work.tile([P, 2048], BF16, name="x_f", bufs=4, align_bytes=64)
-            xf[m] = x_f
-            src = xb[m // 2][:, 2048 * (m % 2) : 2048 * (m % 2) + 2048]
-            if m == 0:
-                nc.scalar.copy(out=x_f[:, 0:1024], in_=src[:, 0:1024].bitcast(FP8))
-                nc.vector.tensor_copy(out=x_f[:, 1024:2048], in_=src[:, 1024:2048].bitcast(FP8))
+        def xs(m, a):
+            x_f = work.tile([P, C], BF16, name="x_f", bufs=6, align_bytes=64)
+            xf[m, a] = x_f
+            first = 2048 * (m % 2) + C * a
+            codes = xb[m // 2][:, first : first + C].bitcast(FP8)
+            if m < 2:
+                nc.scalar.copy(out=x_f[:], in_=codes)
             else:
-                nc.scalar.copy(out=x_f[:], in_=src.bitcast(FP8))
+                nc.vector.tensor_tensor(out=x_f[:], in0=codes, in1=xsc[:], op=ALU.mult)
 
         def tx(m, a):
-            words = xf[m][:].bitcast(F32)
+            words = xf[m, a][:].bitcast(F32)
             x_t = psum.tile([P, 2, G1, P], F32, name="x_t", bufs=2)
             xt[m, a] = x_t
             for g in range(G1):
-                for e in range(2):
-                    base = 512 * a + 256 * g
-                    nc.tensor.transpose(x_t[:, e, g, :], words[:, base + e : base + 256 : 2], ident[:])
+                for u in range(2):
+                    nc.tensor.transpose(x_t[:, u, g, :], words[:, 256 * g + u : 256 * g + 256 : 2], ident[:])
 
-        def xs(m, a):
+        def xw(m, a):
             if m not in xin:
-                x_in = work.tile([P, 2, G1, P, 4], BF16, name="x_in", bufs=3, align_bytes=64)
+                x_in = work.tile([P, 2, G1 * P, 4], BF16, name="x_in", bufs=3, align_bytes=64)
                 xin[m] = x_in
-            nc.vector.tensor_tensor(
-                out=xin[m][:, a].rearrange("p g n (u e) -> p g n u e", u=2),
-                in0=xt[m, a][:].rearrange("p u g n -> p (u g n)").bitcast(BF16).rearrange("p (u g n e) -> p g n u e", u=2, g=G1, e=2),
-                in1=xsc[:].unsqueeze(2).to_broadcast([P, G1, P, 4]).rearrange("p g n (u e) -> p g n u e", u=2),
-                op=ALU.mult,
+            if m < 2:
+                nc.vector.tensor_tensor(
+                    out=xin[m][:, a].rearrange("p (g n) (u e) -> p g n u e", g=G1, u=2),
+                    in0=xt[m, a][:].rearrange("p u g n -> p (u g n)").bitcast(BF16).rearrange("p (u g n e) -> p g n u e", u=2, g=G1, e=2),
+                    in1=xsk[:].unsqueeze(2).to_broadcast([P, G1, P, 4]).rearrange("p g n (u e) -> p g n u e", u=2),
+                    op=ALU.mult,
+                )
+                return
+            nc.scalar.copy(
+                out=xin[m][:, a].rearrange("p n t -> p (n t)").bitcast(F32).rearrange("p (n u) -> p n u", u=2),
+                in_=xt[m, a][:].rearrange("p u g n -> p (g n) u"),
             )
 
         def qx(m, a):
@@ -198,7 +209,7 @@ def tile_multiheadlatentattention_pb_t_w8_kernel(
             nc.vector.quantize_mx(
                 out=x_q[:].rearrange("p a n -> p (a n)").bitcast(FP8X4),
                 scales=x_qs[:].rearrange("p a n -> p (a n)"),
-                in_=xin[m][:].rearrange("p a g n t -> p (a g n t)"),
+                in_=xin[m][:].rearrange("p a n t -> p (a n t)"),
             )
 
         def mx1(m, a):
@@ -209,13 +220,16 @@ def tile_multiheadlatentattention_pb_t_w8_kernel(
                 rt[m] = r_t
             r_out = rt[m][:, a, :]
             for g in range(G1):
-                for out, lo, hi in ((l_t[:], 0, KVL), (r_out, KVL, KVL + R)):
+                for out, words, scales in (
+                    (l_t[:], wa[:, g, 0:KVL], wa_s[4 * g : P, 0:KVL]),
+                    (r_out, wr[:, g].rearrange("p e j -> p (e j)"), wr_s[4 * g : P].rearrange("p e j -> p (e j)")),
+                ):
                     nc.tensor.matmul_mx(
                         out=out,
                         lhsT=xq[m][:, 2 * a + g, :].bitcast(FP8X4),
                         lhsT_scale=xqs[m][:, 2 * a + g, :],
-                        rhs=wa[:, g, lo:hi].bitcast(FP8X4),
-                        rhs_scale=wa_s[4 * g : P, lo:hi],
+                        rhs=words.bitcast(FP8X4),
+                        rhs_scale=scales,
                         start=(g == 0),
                         stop=(g == G1 - 1),
                     )
@@ -229,9 +243,7 @@ def tile_multiheadlatentattention_pb_t_w8_kernel(
             nc.scalar.activation(out=junk[:], in_=lt[m, a][:], func=ACT.Square, accum_out=ssq[m][:, a : a + 1])
 
         def rs(m, a):
-            nc.scalar.activation(
-                out=rstd[m][:, a : a + 1], in_=ssq[m][:, a : a + 1], func=ACT.Abs_reciprocal_sqrt, scale=1.0 / KVL, bias=eps[:]
-            )
+            nc.scalar.activation(out=rstd[m][:], in_=ssq[m][:], func=ACT.Abs_reciprocal_sqrt, scale=1.0 / KVL, bias=eps[:])
 
         def scale_c(m, a):
             if m not in cb:
@@ -291,21 +303,26 @@ def tile_multiheadlatentattention_pb_t_w8_kernel(
             return vs[m]
 
         def evac(m, a, s):
+            copy = nc.vector.tensor_copy if a == 1 and (m >= PAIRS - 3 or (s == 1 and m % 4 == 3)) else nc.scalar.copy
             if s == 0:
-                nc.scalar.copy(out=k_tile(m)[:, a, :, 0:P], in_=kvp[m, a, 0][:].rearrange("p (h d) -> p h d", h=H))
+                copy(out=k_tile(m)[:, a, :, 0:P], in_=kvp[m, a, 0][:].rearrange("p (h d) -> p h d", h=H))
             else:
-                nc.scalar.copy(out=v_tile(m)[:, a, :], in_=kvp[m, a, 1][:])
+                copy(out=v_tile(m)[:, a, :], in_=kvp[m, a, 1][:])
 
-        def store(m):
+        def store_v(m, lo, hi):
             b, q = divmod(m // 2, 2)
-            half = m % 2
+            first = 2 * (m % 2)
             nc.sync.dma_start(
-                out=out_1[b].rearrange("(q p i) h d -> q p (i h d)", q=2, i=4)[q][:, 1024 * half : 1024 * half + 1024],
-                in_=vs[m][:].rearrange("p a n -> p (a n)"),
+                out=out_1[b].rearrange("(q p i) h d -> q p (i h d)", q=2, i=4)[q][:, 512 * (first + lo) : 512 * (first + hi)],
+                in_=vs[m][:, lo:hi, :].rearrange("p a n -> p (a n)"),
             )
+
+        def store_k(m, lo, hi):
+            b, q = divmod(m // 2, 2)
+            first = 2 * (m % 2)
             nc.sync.dma_start(
-                out=out_0[b].rearrange("(q p i) h d -> q p (i h d)", q=2, i=4)[q][:, 2048 * half : 2048 * half + 2048],
-                in_=ks[m][:].rearrange("p a h d -> p (a h d)"),
+                out=out_0[b].rearrange("(q p i) h d -> q p (i h d)", q=2, i=4)[q][:, 1024 * (first + lo) : 1024 * (first + hi)],
+                in_=ks[m][:, lo:hi].rearrange("p a h d -> p (a h d)"),
             )
 
         def rm(m, a):
@@ -314,22 +331,18 @@ def tile_multiheadlatentattention_pb_t_w8_kernel(
             nc.vector.tensor_tensor(
                 out=prod[:],
                 in0=rt[m][:].rearrange("p i d -> p (i d)").unsqueeze(1).to_broadcast([P, 2, 256]),
-                in1=trig[:, m % 4],
+                in1=trig[:, m % 4].rearrange("p w i e j -> p w (i e j)"),
                 op=ALU.mult,
             )
 
         def ra(m, a):
             r_o = work.tile([P, 2, P], F32, name="r_o", bufs=3)
-            nc.vector.tensor_tensor(
-                out=r_o[:].rearrange("p i (j e) -> p (i j) e", e=2),
-                in0=rp[m][:, 0, :].rearrange("p (j e) -> p j e", e=2),
-                in1=rp[m][:, 1, :].rearrange("p (j e) -> p j e", e=2)[:, :, ::-1],
-                op=ALU.add,
-            )
+            planes = [rp[m][:, w, :].rearrange("p (i e j) -> p i e j", i=2, e=2) for w in range(2)]
+            nc.vector.tensor_tensor(out=r_o[:].rearrange("p i (e j) -> p i e j", e=2), in0=planes[0], in1=planes[1][:, :, ::-1, :], op=ALU.add)
             for i in range(2):
                 nc.gpsimd.tensor_scalar(
-                    out=k_tile(m)[:, i, :, P : 2 * P],
-                    in0=r_o[:, i, :].unsqueeze(1).to_broadcast([P, H, P]),
+                    out=k_tile(m)[:, i, :, P : 2 * P].rearrange("p h (j e) -> p h j e", e=2),
+                    in0=r_o[:, i, :].rearrange("p (e j) -> p j e", e=2).unsqueeze(1).to_broadcast([P, H, HALF, 2]),
                     scalar1=1.0,
                     scalar2=0.0,
                     op0=ALU.mult,
@@ -337,7 +350,7 @@ def tile_multiheadlatentattention_pb_t_w8_kernel(
                 )
 
         step = {
-            "castp": cast, "tx": tx, "xs": xs, "qxp": qx, "mx1": mx1, "sq": sq, "rs": rs, "c": scale_c, "tc": tcc, "ccp": copy_c, "qcp": qc, "rm": rm, "ra": ra,
+            "tx": tx, "xs": xs, "xw": xw, "qxp": qx, "mx1": mx1, "sq": sq, "rsp": rs, "c": scale_c, "tc": tcc, "ccp": copy_c, "qcp": qc, "rm": rm, "ra": ra,
             "m2A": lambda m, a: mx2(m, a, 0), "m2B": lambda m, a: mx2(m, a, 1), "evA": lambda m, a: evac(m, a, 0), "evB": lambda m, a: evac(m, a, 1),
         }
         lead = max(lag for _, _, lag in ORDER)
@@ -349,8 +362,13 @@ def tile_multiheadlatentattention_pb_t_w8_kernel(
                     continue
                 step[name](m, a)
                 if name in ("evA", "evB"):
-                    evs[m] = evs.get(m, 0) + 1
-                    if evs[m] == 4:
-                        store(m)
-                if name == "xs" and m == 0 and a == 1:
-                    tables()
+                    store = store_k if name == "evA" else store_v
+                    evs[name, m] = evs.get((name, m), 0) + 1
+                    if m == PAIRS - 1:
+                        store(m, a, a + 1)
+                    elif evs[name, m] == 2:
+                        store(m, 0, 2)
+                if (name, m, a) == ("xs", 1, 1):
+                    trig_tables()
+                if (name, m, a) == ("xw", 0, 1):
+                    planar_rope_weights()

import math
from contextlib import ExitStack

import concourse.mybir as mybir
from concourse.masks import make_identity

F32 = mybir.dt.float32
BF16 = mybir.dt.bfloat16
I32 = mybir.dt.int32
U32 = mybir.dt.uint32
U8 = mybir.dt.uint8
FP8 = mybir.dt.float8_e4m3fn
FP8X4 = mybir.dt.float8_e4m3fn_x4
ACT = mybir.ActivationFunctionType
ALU = mybir.AluOpType

B, T, C, H, R, KVL, VD = 4, 1024, 1024, 4, 128, 512, 128
THETA = 10000.0
EPS = 1e-6
HALF = R // 2
FLOPS = 2 * B * T * (C * (KVL + R) + KVL * H * (R + VD))

P = 128
PAIRS = 16
G1 = C // 512

ORDER = (
    ("ra", 0, 1),
    ("tc", 1, 2),
    ("qxp", 0, 4),
    ("evB", 1, 1),
    ("rsp", 0, 3),
    ("m2A", 1, 1),
    ("evA", 0, 1),
    ("xw", 0, 5),
    ("rm", 0, 3),
    ("m2B", 0, 1),
    ("ccp", 0, 2),
    ("c", 0, 3),
    ("c", 1, 3),
    ("xs", 0, 6),
    ("tx", 1, 5),
    ("evA", 1, 1),
    ("evB", 0, 1),
    ("mx1", 0, 4),
    ("mx1", 1, 4),
    ("xw", 1, 5),
    ("sq", 0, 4),
    ("tc", 0, 3),
    ("qcp", 0, 2),
    ("m2B", 1, 2),
    ("m2A", 0, 2),
    ("sq", 1, 4),
    ("xs", 1, 6),
    ("tx", 0, 6),
)


def tile_multiheadlatentattention_pb_t_w8_kernel(
    tc, x_bytes, x_scale, w_kva_words, w_kva_scales, kva_norm_w, w_kvb_words, w_kvb_scales, out_0, out_1
):
    nc = tc.nc
    with ExitStack() as ctx:
        const = ctx.enter_context(tc.tile_pool(name="const", bufs=1))
        work = ctx.enter_context(tc.tile_pool(name="work", bufs=2))
        psum = ctx.enter_context(tc.psum_pool(name="psum", bufs=1))
        ctx.enter_context(tc.manual_schedule())

        xb = []
        for g in range(8):
            xbg = const.tile([P, 4096], U8, name=f"xbytes{g}", align_bytes=64)
            xb.append(xbg)
        wa = const.tile([P, G1, KVL + R], U32, name="wa", align_bytes=64)
        wa_s = const.tile([P, KVL + R], U8, name="wa_s", align_bytes=64)
        wr = const.tile([P, G1, 2, HALF], U32, name="wr", align_bytes=64)
        wr_s = const.tile([P, 2, HALF], U8, name="wr_s", align_bytes=64)
        wb = const.tile([P, 2, 512], U32, name="wb", align_bytes=64)
        wb_s = const.tile([P, 2, 512], U8, name="wb_s", align_bytes=64)
        xsc = const.tile([P, C], F32, name="xsc", align_bytes=64)
        xsk = const.tile([P, G1, 4], F32, name="xsk", align_bytes=64)
        gain = const.tile([P, KVL], BF16, name="gain", align_bytes=64)
        ident = const.tile([P, P], F32, name="ident", align_bytes=64)
        eps = const.tile([P, 1], F32, name="eps", align_bytes=64)
        warm = const.tile([P, 1], F32, name="warm", align_bytes=64)

        def x_src(g):
            b, q = divmod(g, 2)
            return x_bytes[b].rearrange("(q p i) k -> q p (i k)", q=2, i=4)[q]

        nc.gpsimd.memset(wa_s[:].bitcast(I32), 0)
        nc.gpsimd.memset(wb_s[:].rearrange("p s n -> p (s n)").bitcast(I32), 0)
        nc.vector.memset(eps[:], EPS)
        nc.vector.memset(warm[:], 0.0)
        nc.scalar.dma_start(out=xsk[:], in_=x_scale.rearrange("a b (g p t) -> p (a b g) t", g=G1, t=4))
        nc.sync.dma_start(out=xb[0][:, 0:1024], in_=x_src(0)[:, 0:1024])
        nc.sync.dma_start(out=xb[0][:, 1024:2048], in_=x_src(0)[:, 1024:2048])
        for qd in range(4):
            nc.sync.dma_start(
                out=wa_s[32 * qd : 32 * qd + 8, :].bitcast(I32),
                in_=w_kva_scales[:, 4 * qd : 4 * qd + 4, :].bitcast(I32),
            )
        for g in range(G1):
            nc.sync.dma_start(out=wa[:, g, :].bitcast(I32), in_=w_kva_words[g].rearrange("p n t -> p (n t)").bitcast(I32))
        nc.sync.dma_start(out=xb[0][:, 2048:4096], in_=x_src(0)[:, 2048:4096])
        nc.sync.dma_start(out=xb[1][:], in_=x_src(1))
        nc.sync.dma_start(out=xsc[:], in_=x_scale.rearrange("a b k -> (a b k)").partition_broadcast(P))
        nc.sync.dma_start(out=gain[:], in_=kva_norm_w.partition_broadcast(P))
        for qd in range(4):
            for s in range(2):
                nc.sync.dma_start(
                    out=wb_s[32 * qd : 32 * qd + 4, s, :].bitcast(I32).rearrange("p (h d) -> p h d", h=H),
                    in_=w_kvb_scales[0][4 * qd : 4 * qd + 4, :].bitcast(I32).rearrange("r (h s d) -> r s h d", h=H, s=2)[:, s],
                )
        for s in range(2):
            nc.sync.dma_start(
                out=wb[:, s, :].bitcast(I32).rearrange("p (h d) -> p h d", h=H),
                in_=w_kvb_words[0].rearrange("p n t -> p (n t)").bitcast(I32).rearrange("p (h s d) -> p s h d", h=H, s=2)[:, s],
            )
        for g in range(2, 8):
            nc.sync.dma_start(out=xb[g][:], in_=x_src(g))

        u = const.tile([P, HALF], F32, name="u")
        tpos = const.tile([P, 8], F32, name="tpos")
        turns = const.tile([P, 8, HALF], F32, name="turns")
        whole = const.tile([P, 8, HALF], I32, name="whole")
        half = const.tile([P, 8, HALF], F32, name="half")
        half2 = const.tile([P, 8, HALF], F32, name="half2")
        trig = const.tile([P, 4, 2, 2, 2, HALF], F32, name="trig")
        nc.gpsimd.iota(tpos[:], pattern=[[512, 2], [1, 4]], base=0, channel_multiplier=4, allow_small_or_imprecise_dtypes=True)
        nc.gpsimd.tensor_scalar(out=tpos[:], in0=tpos[:], scalar1=1.0 / (2.0 * math.pi), scalar2=0.0, op0=ALU.mult, op1=ALU.add)
        make_identity(nc, ident[:])
        nc.vector.memset(u[:, 0:1], 1.0)
        n = 1
        while n < HALF:
            nc.vector.tensor_scalar(out=u[:, n : 2 * n], in0=u[:, 0:n], scalar1=THETA ** (-n / HALF), scalar2=None, op0=ALU.mult)
            n *= 2
        nc.vector.tensor_tensor(
            out=turns[:], in0=tpos[:].unsqueeze(2).to_broadcast([P, 8, HALF]), in1=u[:].unsqueeze(1).to_broadcast([P, 8, HALF]), op=ALU.mult
        )
        nc.vector.tensor_copy(out=whole[:], in_=turns[:])
        nc.vector.tensor_tensor(out=turns[:], in0=turns[:], in1=whole[:], op=ALU.subtract)
        nc.scalar.activation(out=warm[:], in_=warm[:], func=ACT.Sin)

        def trig_tables():
            by_pair = turns[:].rearrange("p (s i) j -> p s i j", i=2)
            for e, sign in ((0, 1.0), (1, -1.0)):
                nc.scalar.activation(out=trig[:, :, 1, :, e, :], in_=by_pair, func=ACT.Sin, scale=sign * 2.0 * math.pi)
            nc.scalar.activation(out=half[:], in_=turns[:], func=ACT.Sin, scale=math.pi)
            nc.scalar.activation(out=half2[:], in_=half[:], func=ACT.Square)
            nc.scalar.activation(
                out=trig[:, :, 0],
                in_=half2[:].rearrange("p (s i) j -> p s i j", i=2).unsqueeze(3).to_broadcast([P, 4, 2, 2, HALF]),
                func=ACT.Copy,
                scale=-2.0,
                bias=1.0,
            )
            nc.scalar.activation(out=warm[:], in_=warm[:], func=ACT.Abs_reciprocal_sqrt, bias=eps[:])

        def planar_rope_weights():
            nc.vector.tensor_copy(out=wr[:].bitcast(I32), in_=wa[:].bitcast(I32)[:, :, KVL:].rearrange("p g (j e) -> p g e j", e=2))
            nc.vector.tensor_copy(out=wr_s[:], in_=wa_s[:, KVL:].rearrange("p (j e) -> p e j", e=2))

        xf, xt, xin, xq, xqs = {}, {}, {}, {}, {}
        lt, rt, cb, ssq, rstd, ct, cin, cq, cqs = {}, {}, {}, {}, {}, {}, {}, {}, {}
        kvp, rp, ks, vs = {}, {}, {}, {}

        def ok(m):
            return 0 <= m < PAIRS

        def xs(m, a):
            x_f = work.tile([P, C], BF16, name="x_f", bufs=6, align_bytes=64)
            xf[m, a] = x_f
            first = 2048 * (m % 2) + C * a
            codes = xb[m // 2][:, first : first + C].bitcast(FP8)
            if m < 2:
                nc.scalar.copy(out=x_f[:], in_=codes)
            else:
                nc.vector.tensor_tensor(out=x_f[:], in0=codes, in1=xsc[:], op=ALU.mult)

        def tx(m, a):
            words = xf[m, a][:].bitcast(F32)
            x_t = psum.tile([P, 2, G1, P], F32, name="x_t", bufs=2)
            xt[m, a] = x_t
            for g in range(G1):
                for u in range(2):
                    nc.tensor.transpose(x_t[:, u, g, :], words[:, 256 * g + u : 256 * g + 256 : 2], ident[:])

        def xw(m, a):
            if m not in xin:
                x_in = work.tile([P, 2, G1 * P, 4], BF16, name="x_in", bufs=3, align_bytes=64)
                xin[m] = x_in
            if m < 2:
                nc.vector.tensor_tensor(
                    out=xin[m][:, a].rearrange("p (g n) (u e) -> p g n u e", g=G1, u=2),
                    in0=xt[m, a][:].rearrange("p u g n -> p (u g n)").bitcast(BF16).rearrange("p (u g n e) -> p g n u e", u=2, g=G1, e=2),
                    in1=xsk[:].unsqueeze(2).to_broadcast([P, G1, P, 4]).rearrange("p g n (u e) -> p g n u e", u=2),
                    op=ALU.mult,
                )
                return
            nc.scalar.copy(
                out=xin[m][:, a].rearrange("p n t -> p (n t)").bitcast(F32).rearrange("p (n u) -> p n u", u=2),
                in_=xt[m, a][:].rearrange("p u g n -> p (g n) u"),
            )

        def qx(m, a):
            x_q = work.tile([P, 4, P], U32, name="x_q", bufs=3, align_bytes=64)
            x_qs = work.tile([P, 4, P], U8, name="x_qs", bufs=3, align_bytes=64)
            xq[m], xqs[m] = x_q, x_qs
            nc.vector.quantize_mx(
                out=x_q[:].rearrange("p a n -> p (a n)").bitcast(FP8X4),
                scales=x_qs[:].rearrange("p a n -> p (a n)"),
                in_=xin[m][:].rearrange("p a n t -> p (a n t)"),
            )

        def mx1(m, a):
            l_t = psum.tile([P, 512], F32, name="l_t", bufs=2)
            lt[m, a] = l_t
            if m not in rt:
                r_t = psum.tile([P, 2, P], F32, name="r_t", bufs=1)
                rt[m] = r_t
            r_out = rt[m][:, a, :]
            for g in range(G1):
                for out, words, scales in (
                    (l_t[:], wa[:, g, 0:KVL], wa_s[4 * g : P, 0:KVL]),
                    (r_out, wr[:, g].rearrange("p e j -> p (e j)"), wr_s[4 * g : P].rearrange("p e j -> p (e j)")),
                ):
                    nc.tensor.matmul_mx(
                        out=out,
                        lhsT=xq[m][:, 2 * a + g, :].bitcast(FP8X4),
                        lhsT_scale=xqs[m][:, 2 * a + g, :],
                        rhs=words.bitcast(FP8X4),
                        rhs_scale=scales,
                        start=(g == 0),
                        stop=(g == G1 - 1),
                    )

        def sq(m, a):
            if m not in ssq:
                s_s = work.tile([P, 2], F32, name="s_s", bufs=3)
                r_s = work.tile([P, 2], F32, name="r_s", bufs=3)
                ssq[m], rstd[m] = s_s, r_s
            junk = work.tile([P, 512], BF16, name="junk", bufs=2)
            nc.scalar.activation(out=junk[:], in_=lt[m, a][:], func=ACT.Square, accum_out=ssq[m][:, a : a + 1])

        def rs(m, a):
            nc.scalar.activation(out=rstd[m][:], in_=ssq[m][:], func=ACT.Abs_reciprocal_sqrt, scale=1.0 / KVL, bias=eps[:])

        def scale_c(m, a):
            if m not in cb:
                c_b = work.tile([P, 1024], BF16, name="c_b", bufs=3, align_bytes=64)
                cb[m] = c_b
            nc.vector.scalar_tensor_tensor(
                out=cb[m][:, 512 * a : 512 * a + 512], in0=lt[m, a][:], scalar=rstd[m][:, a : a + 1], in1=gain[:], op0=ALU.mult, op1=ALU.mult
            )

        def tcc(m, a):
            words = cb[m][:].bitcast(F32)
            if m not in ct:
                c_t = psum.tile([P, 4, P], F32, name="c_t", bufs=1)
                ct[m] = c_t
            for e in range(2):
                nc.tensor.transpose(ct[m][:, 2 * a + e, :], words[:, 256 * a + e : 256 * a + 256 : 2], ident[:])

        def copy_c(m, a):
            c_in = work.tile([P, 1024], BF16, name="c_in", bufs=3, align_bytes=64)
            nc.scalar.copy(
                out=c_in[:].bitcast(F32).rearrange("p (a n u) -> p a n u", a=2, u=2),
                in_=ct[m][:].rearrange("p (a u) n -> p a n u", a=2),
            )
            cin[m] = c_in

        def qc(m, a):
            c_q = work.tile([P, 2, P], U32, name="c_q", bufs=3, align_bytes=64)
            c_qs = work.tile([P, 2, P], U8, name="c_qs", bufs=3, align_bytes=64)
            cq[m], cqs[m] = c_q, c_qs
            nc.vector.quantize_mx(
                out=c_q[:].rearrange("p a n -> p (a n)").bitcast(FP8X4), scales=c_qs[:].rearrange("p a n -> p (a n)"), in_=cin[m][:]
            )

        def mx2(m, a, s):
            kv = psum.tile([P, 512], F32, name="kv", bufs=2)
            kvp[m, a, s] = kv
            nc.tensor.matmul_mx(
                out=kv[:],
                lhsT=cq[m][:, a, :].bitcast(FP8X4),
                lhsT_scale=cqs[m][:, a, :],
                rhs=wb[:, s, :].bitcast(FP8X4),
                rhs_scale=wb_s[:, s, :],
                start=True,
                stop=True,
            )

        def k_tile(m):
            if m not in ks:
                k_s = work.tile([P, 2, H, 2 * P], F32, name="k_s", bufs=4)
                ks[m] = k_s
            return ks[m]

        def v_tile(m):
            if m not in vs:
                v_s = work.tile([P, 2, 512], F32, name="v_s", bufs=4)
                vs[m] = v_s
            return vs[m]

        def evac(m, a, s):
            copy = nc.vector.tensor_copy if a == 1 and (m >= PAIRS - 3 or (s == 1 and m % 4 == 3)) else nc.scalar.copy
            if s == 0:
                copy(out=k_tile(m)[:, a, :, 0:P], in_=kvp[m, a, 0][:].rearrange("p (h d) -> p h d", h=H))
            else:
                copy(out=v_tile(m)[:, a, :], in_=kvp[m, a, 1][:])

        def store_v(m, lo, hi):
            b, q = divmod(m // 2, 2)
            first = 2 * (m % 2)
            nc.sync.dma_start(
                out=out_1[b].rearrange("(q p i) h d -> q p (i h d)", q=2, i=4)[q][:, 512 * (first + lo) : 512 * (first + hi)],
                in_=vs[m][:, lo:hi, :].rearrange("p a n -> p (a n)"),
            )

        def store_k(m, lo, hi):
            b, q = divmod(m // 2, 2)
            first = 2 * (m % 2)
            nc.sync.dma_start(
                out=out_0[b].rearrange("(q p i) h d -> q p (i h d)", q=2, i=4)[q][:, 1024 * (first + lo) : 1024 * (first + hi)],
                in_=ks[m][:, lo:hi].rearrange("p a h d -> p (a h d)"),
            )

        def rm(m, a):
            prod = work.tile([P, 2, 256], F32, name="prod", bufs=3)
            rp[m] = prod
            nc.vector.tensor_tensor(
                out=prod[:],
                in0=rt[m][:].rearrange("p i d -> p (i d)").unsqueeze(1).to_broadcast([P, 2, 256]),
                in1=trig[:, m % 4].rearrange("p w i e j -> p w (i e j)"),
                op=ALU.mult,
            )

        def ra(m, a):
            r_o = work.tile([P, 2, P], F32, name="r_o", bufs=3)
            planes = [rp[m][:, w, :].rearrange("p (i e j) -> p i e j", i=2, e=2) for w in range(2)]
            nc.vector.tensor_tensor(out=r_o[:].rearrange("p i (e j) -> p i e j", e=2), in0=planes[0], in1=planes[1][:, :, ::-1, :], op=ALU.add)
            for i in range(2):
                nc.gpsimd.tensor_scalar(
                    out=k_tile(m)[:, i, :, P : 2 * P].rearrange("p h (j e) -> p h j e", e=2),
                    in0=r_o[:, i, :].rearrange("p (e j) -> p j e", e=2).unsqueeze(1).to_broadcast([P, H, HALF, 2]),
                    scalar1=1.0,
                    scalar2=0.0,
                    op0=ALU.mult,
                    op1=ALU.add,
                )

        step = {
            "tx": tx, "xs": xs, "xw": xw, "qxp": qx, "mx1": mx1, "sq": sq, "rsp": rs, "c": scale_c, "tc": tcc, "ccp": copy_c, "qcp": qc, "rm": rm, "ra": ra,
            "m2A": lambda m, a: mx2(m, a, 0), "m2B": lambda m, a: mx2(m, a, 1), "evA": lambda m, a: evac(m, a, 0), "evB": lambda m, a: evac(m, a, 1),
        }
        lead = max(lag for _, _, lag in ORDER)
        evs = {}
        for it in range(-lead, PAIRS):
            for name, a, lag in ORDER:
                m = it + lag
                if not ok(m):
                    continue
                step[name](m, a)
                if name in ("evA", "evB"):
                    store = store_k if name == "evA" else store_v
                    evs[name, m] = evs.get((name, m), 0) + 1
                    if m == PAIRS - 1:
                        store(m, a, a + 1)
                    elif evs[name, m] == 2:
                        store(m, 0, 2)
                if (name, m, a) == ("xs", 1, 1):
                    trig_tables()
                if (name, m, a) == ("xw", 0, 1):
                    planar_rope_weights()
